import numpy as np
import ml_dtypes


def mxq(x, axis, fmt="e4m3"):
    dtype, down = {"e4m3": (ml_dtypes.float8_e4m3fn, 7), "e5m2": (ml_dtypes.float8_e5m2, 14)}[fmt]
    v = np.moveaxis(np.asarray(x, np.float32).astype(ml_dtypes.bfloat16).astype(np.float64), axis, -1)
    blocks = v.reshape(v.shape[:-1] + (-1, 32))
    amax = np.abs(blocks).max(-1, keepdims=True)
    byte = np.maximum(np.where(amax > 0, np.frexp(amax)[1] - 1 + 127, 0) - down, 1)
    scale = np.exp2(byte - 127.0)
    codes = (blocks / scale).astype(np.float32).astype(dtype).astype(np.float64)
    return np.moveaxis((codes * scale).reshape(v.shape), -1, axis)


WIDE = False


def mx_kscale(k):
    if not WIDE:
        return np.ones(k)
    levels = np.array([10, -10, 5, -5, 0])
    if k % 512:
        return np.exp2(np.random.permutation(np.resize(levels, k // 32))).repeat(32)
    a = np.empty((k // 512, 16))
    for p in range(k // 512):
        a[p, :8] = np.random.permutation(np.resize(levels, 8))
        for g in range(8):
            far = levels[np.abs(levels - a[p, g]) >= 10]
            a[p, g + 8] = far[np.random.randint(len(far))]
    return np.exp2(a.ravel()).repeat(32)


BF16 = ml_dtypes.bfloat16


def bf(x):
    return np.asarray(x, np.float32).astype(BF16)


def f64(x):
    return np.asarray(x).astype(np.float64)


N, MI, MO, LMAX = 1024, 512, 128, 3
C = (LMAX + 1) ** 2


def setup_inputs():
    s = mx_kscale(MI)
    d = {"x": bf(np.random.standard_normal((N, MI, C)) * s[None, :, None])}
    for l in range(LMAX + 1):
        d["w%d" % l] = bf(np.random.standard_normal((MI, MO)) / np.sqrt(MI) / s[:, None])
    return d


def reference(x, w0, w1, w2, w3):
    xq = mxq(f64(x), 1, "e4m3")
    parts = []
    for l, w in enumerate([w0, w1, w2, w3]):
        xl = xq[:, :, l * l:(l + 1) ** 2].transpose(0, 2, 1)
        parts.append((xl @ mxq(f64(w), 0, "e4m3")).transpose(0, 2, 1))
    return np.concatenate(parts, axis=2)

@@ -1,0 +1,162 @@
+from contextlib import ExitStack
+
+import concourse.mybir as mybir
+from concourse.masks import make_identity
+
+F32 = mybir.dt.float32
+BF16 = mybir.dt.bfloat16
+U32 = mybir.dt.uint32
+U8 = mybir.dt.uint8
+FP8X4 = mybir.dt.float8_e4m3fn_x4
+ALU = mybir.AluOpType
+
+P = 128
+N, MI, MO, C = 1024, 512, 128, 16
+PACK = 4
+NT = N // P
+DEGREE = [0, 1, 1, 1, 2, 2, 2, 2, 2, 3, 3, 3, 3, 3, 3, 3]
+BANK = 2 * P * PACK
+
+FLOPS = 2 * N * C * MI * MO
+
+UNITS = [(m, 4 * h, 4) for m in range(NT - 1) for h in range(2)] + [(NT - 1, 0, 4), (NT - 1, 4, 2), (NT - 1, 6, 2)]
+
+
+def tile_irrepsstridelinear_kernel(tc, x, w0, w1, w2, w3, out):
+    nc = tc.nc
+    with ExitStack() as ctx:
+        ctx.enter_context(tc.manual_schedule())
+        const = ctx.enter_context(tc.tile_pool(name="const", bufs=1))
+        xpool = ctx.enter_context(tc.tile_pool(name="xpool", bufs=1))
+        gpool = ctx.enter_context(tc.tile_pool(name="gpool", bufs=3))
+        qpool = ctx.enter_context(tc.tile_pool(name="qpool", bufs=3))
+        opool = ctx.enter_context(tc.tile_pool(name="opool", bufs=5))
+        tps = ctx.enter_context(tc.psum_pool(name="tps", bufs=6))
+        ops = ctx.enter_context(tc.psum_pool(name="ops", bufs=2))
+
+        xs = []
+        wraw = const.tile([P, 4, PACK, MO], BF16, name="wraw")
+        for m in range(NT):
+            xt = xpool.tile([P, MI * C], BF16, name="x%d" % m)
+            rows = x[m * P:(m + 1) * P].rearrange("n i c -> n (i c)")
+            pieces = PACK if m == 0 else 1
+            wide = MI * C // pieces
+            for t in range(pieces):
+                nc.sync.dma_start(out=xt[:, t * wide:(t + 1) * wide], in_=rows[:, t * wide:(t + 1) * wide])
+            xs.append(xt)
+            if m == 0:
+                for l, w in enumerate([w0, w1, w2, w3]):
+                    nc.sync.dma_start(out=wraw[:, l], in_=w.rearrange("(p j) o -> p j o", j=PACK))
+
+        ident = const.tile([P, P], F32, name="ident")
+        make_identity(nc, ident[:])
+
+        wgrp = const.tile([P, 4, MO, PACK], BF16, name="wgrp", align_bytes=64)
+        wcodes = const.tile([P, 4 * MO], U32, name="wcodes", align_bytes=64)
+        wscales = const.tile([P, 4 * MO], U8, name="wscales", align_bytes=64)
+        nc.gpsimd.tensor_scalar(
+            out=wgrp[:], in0=wraw[:].rearrange("p l j o -> p l o j"),
+            scalar1=1.0, scalar2=0.0, op0=ALU.mult, op1=ALU.add)
+
+        def quantise_weights():
+            nc.vector.quantize_mx(
+                out=wcodes[:].bitcast(FP8X4),
+                scales=wscales[:],
+                in_=wgrp[:].rearrange("p l o j -> p (l o j)"),
+            )
+
+        banks = {}
+        grouped = {}
+        quant = {}
+        accs = {}
+        staged = {}
+
+        def transposes(u):
+            m, cp0, nb = UNITS[u]
+            words = xs[m][:].bitcast(F32)
+            for b in range(nb):
+                banks[(u, b)] = tps.tile([P, PACK * P], F32, name="bank", tag="bank")
+            order = [(b, t) for b in range(nb) for t in range(PACK)]
+            if u == 0:
+                order = [(b, t) for t in range(PACK) for b in range(nb)]
+            for b, t in order:
+                first = 8 * t + cp0 + b
+                nc.tensor.transpose(
+                    banks[(u, b)][:, t * P:(t + 1) * P],
+                    words[:, first:first + 8 * PACK * (P - 1) + 1:8 * PACK],
+                    ident[:],
+                )
+
+        def regroup(u):
+            m, cp0, nb = UNITS[u]
+            g = gpool.tile([P, 4 * BANK], BF16, name="g", tag="g", align_bytes=64)
+            grouped[u] = g
+            for b in range(nb):
+                src = banks[(u, b)][:].bitcast(BF16).rearrange(
+                    "p (t n e) -> p e n t", t=PACK, n=P, e=2)
+                dst = g[:, b * BANK:(b + 1) * BANK].rearrange(
+                    "p (e n t) -> p e n t", e=2, n=P, t=PACK)
+                if b % 2 == 0:
+                    nc.vector.tensor_copy(out=dst, in_=src)
+                else:
+                    nc.scalar.copy(out=dst, in_=src)
+
+        def quantise(u):
+            m, cp0, nb = UNITS[u]
+            codes = qpool.tile([P, BANK], U32, name="codes", tag="codes", align_bytes=64)
+            scales = qpool.tile([P, BANK], U8, name="scales", tag="scales", align_bytes=64)
+            wide = nb * BANK // PACK
+            nc.vector.quantize_mx(
+                out=codes[:, :wide].bitcast(FP8X4), scales=scales[:, :wide],
+                in_=grouped[u][:, :nb * BANK])
+            quant[u] = (codes, scales)
+
+        def multiply(u):
+            m, cp0, nb = UNITS[u]
+            codes, scales = quant[u]
+            for b in range(nb // 2):
+                acc = ops.tile([P, 4 * MO], F32, name="acc", tag="acc")
+                for cc in range(4):
+                    cl = 4 * b + cc
+                    l = DEGREE[2 * cp0 + cl]
+                    nc.tensor.matmul_mx(
+                        out=acc[:, cc * MO:(cc + 1) * MO],
+                        lhsT=codes[:, cl * P:(cl + 1) * P].bitcast(FP8X4),
+                        lhsT_scale=scales[:, cl * P:(cl + 1) * P],
+                        rhs=wcodes[:, l * MO:(l + 1) * MO].bitcast(FP8X4),
+                        rhs_scale=wscales[:, l * MO:(l + 1) * MO],
+                        start=True,
+                        stop=True,
+                    )
+                accs[(u, b)] = acc
+
+        def drain(u):
+            m, cp0, nb = UNITS[u]
+            if cp0 == 0:
+                staged[m] = opool.tile([P, MO * C], F32, name="osb", tag="osb")
+            osb = staged[m]
+            view = osb[:].rearrange("p (o c) -> p o c", c=C)
+            for b in range(nb // 2):
+                c0 = 2 * cp0 + 4 * b
+                nc.scalar.copy(
+                    out=view[:, :, c0:c0 + 4],
+                    in_=accs[(u, b)][:].rearrange("p (cc o) -> p o cc", cc=4),
+                )
+            if cp0 + nb == C // 2:
+                nc.sync.dma_start(
+                    out=out[m * P:(m + 1) * P].rearrange("n o c -> n (o c)"), in_=osb[:])
+
+        count = len(UNITS)
+        transposes(0)
+        for k in range(count + 2):
+            if k < count:
+                regroup(k)
+            if k + 1 < count:
+                transposes(k + 1)
+            if k == 1:
+                quantise_weights()
+            if 0 <= k - 1 < count:
+                quantise(k - 1)
+                multiply(k - 1)
+            if 0 <= k - 2 < count:
+                drain(k - 2)

@@ -15,6 +15,8 @@ N, MI, MO, C = 1024, 512, 128, 16
 PACK = 4
 NT = N // P
 DEGREE = [0, 1, 1, 1, 2, 2, 2, 2, 2, 3, 3, 3, 3, 3, 3, 3]
+FIRST_PAIRED = 2
+AHEAD = 3
 BANK = 2 * P * PACK
 
 FLOPS = 2 * N * C * MI * MO
@@ -29,6 +31,7 @@ def tile_irrepsstridelinear_kernel(tc, x, w0, w1, w2, w3, out):
         const = ctx.enter_context(tc.tile_pool(name="const", bufs=1))
         xpool = ctx.enter_context(tc.tile_pool(name="xpool", bufs=1))
         gpool = ctx.enter_context(tc.tile_pool(name="gpool", bufs=3))
+        ppool = ctx.enter_context(tc.tile_pool(name="ppool", bufs=6))
         qpool = ctx.enter_context(tc.tile_pool(name="qpool", bufs=3))
         opool = ctx.enter_context(tc.tile_pool(name="opool", bufs=5))
         tps = ctx.enter_context(tc.psum_pool(name="tps", bufs=6))
@@ -39,10 +42,7 @@ def tile_irrepsstridelinear_kernel(tc, x, w0, w1, w2, w3, out):
         for m in range(NT):
             xt = xpool.tile([P, MI * C], BF16, name="x%d" % m)
             rows = x[m * P:(m + 1) * P].rearrange("n i c -> n (i c)")
-            pieces = PACK if m == 0 else 1
-            wide = MI * C // pieces
-            for t in range(pieces):
-                nc.sync.dma_start(out=xt[:, t * wide:(t + 1) * wide], in_=rows[:, t * wide:(t + 1) * wide])
+            nc.sync.dma_start(out=xt[:], in_=rows)
             xs.append(xt)
             if m == 0:
                 for l, w in enumerate([w0, w1, w2, w3]):
@@ -71,32 +71,47 @@ def tile_irrepsstridelinear_kernel(tc, x, w0, w1, w2, w3, out):
         accs = {}
         staged = {}
 
+        paired = {}
+
+        def pair_up(u):
+            m, cp0, nb = UNITS[u]
+            cp = cp0 + nb - 1
+            pt = ppool.tile([P, 2, 2, P, 2], BF16, name="pairs", tag="pairs")
+            src = xs[m][:].rearrange("n (p v s c) -> n c v p s", v=2, s=2, c=C)
+            for e in range(2):
+                nc.gpsimd.tensor_scalar(
+                    out=pt[:, e], in0=src[:, 2 * cp + e],
+                    scalar1=1.0, scalar2=0.0, op0=ALU.mult, op1=ALU.add)
+            paired[u] = pt
+
         def transposes(u):
             m, cp0, nb = UNITS[u]
             words = xs[m][:].bitcast(F32)
             for b in range(nb):
-                banks[(u, b)] = tps.tile([P, PACK * P], F32, name="bank", tag="bank")
-            order = [(b, t) for b in range(nb) for t in range(PACK)]
-            if u == 0:
-                order = [(b, t) for t in range(PACK) for b in range(nb)]
-            for b, t in order:
-                first = 8 * t + cp0 + b
-                nc.tensor.transpose(
-                    banks[(u, b)][:, t * P:(t + 1) * P],
-                    words[:, first:first + 8 * PACK * (P - 1) + 1:8 * PACK],
-                    ident[:],
-                )
+                bank = tps.tile([P, PACK * P], F32, name="bank", tag="bank")
+                banks[(u, b)] = bank
+                for t in range(PACK):
+                    if u in paired and b == nb - 1:
+                        src = paired[u][:].rearrange("n e v p s -> n (e v p s)").bitcast(F32)[:, t * P:(t + 1) * P]
+                    else:
+                        first = 8 * t + cp0 + b
+                        src = words[:, first:first + 8 * PACK * (P - 1) + 1:8 * PACK]
+                    nc.tensor.transpose(bank[:, t * P:(t + 1) * P], src, ident[:])
 
         def regroup(u):
             m, cp0, nb = UNITS[u]
             g = gpool.tile([P, 4 * BANK], BF16, name="g", tag="g", align_bytes=64)
             grouped[u] = g
             for b in range(nb):
-                src = banks[(u, b)][:].bitcast(BF16).rearrange(
-                    "p (t n e) -> p e n t", t=PACK, n=P, e=2)
-                dst = g[:, b * BANK:(b + 1) * BANK].rearrange(
-                    "p (e n t) -> p e n t", e=2, n=P, t=PACK)
-                if b % 2 == 0:
+                part = g[:, b * BANK:(b + 1) * BANK]
+                if u in paired and b == nb - 1:
+                    src = banks[(u, b)][:].rearrange("p (e v n) -> p e n v", e=2, v=2)
+                    dst = part.bitcast(F32).rearrange("p (e n v) -> p e n v", e=2, v=2)
+                else:
+                    src = banks[(u, b)][:].bitcast(BF16).rearrange(
+                        "p (t n e) -> p e n t", t=PACK, n=P, e=2)
+                    dst = part.rearrange("p (e n t) -> p e n t", e=2, n=P, t=PACK)
+                if (b + u) % 2 == 0:
                     nc.vector.tensor_copy(out=dst, in_=src)
                 else:
                     nc.scalar.copy(out=dst, in_=src)
@@ -148,7 +163,11 @@ def tile_irrepsstridelinear_kernel(tc, x, w0, w1, w2, w3, out):
 
         count = len(UNITS)
         transposes(0)
+        for k in range(FIRST_PAIRED, FIRST_PAIRED + AHEAD):
+            pair_up(k)
         for k in range(count + 2):
+            if FIRST_PAIRED + AHEAD <= k + 1 + AHEAD < count and k > 0:
+                pair_up(k + 1 + AHEAD)
             if k < count:
                 regroup(k)
             if k + 1 < count:

@@ -15,7 +15,6 @@ N, MI, MO, C = 1024, 512, 128, 16
 PACK = 4
 NT = N // P
 DEGREE = [0, 1, 1, 1, 2, 2, 2, 2, 2, 3, 3, 3, 3, 3, 3, 3]
-FIRST_PAIRED = 2
 AHEAD = 3
 BANK = 2 * P * PACK
 
@@ -32,6 +31,7 @@ def tile_irrepsstridelinear_kernel(tc, x, w0, w1, w2, w3, out):
         xpool = ctx.enter_context(tc.tile_pool(name="xpool", bufs=1))
         gpool = ctx.enter_context(tc.tile_pool(name="gpool", bufs=3))
         ppool = ctx.enter_context(tc.tile_pool(name="ppool", bufs=6))
+        gates = ctx.enter_context(tc.tile_pool(name="gates", bufs=4))
         qpool = ctx.enter_context(tc.tile_pool(name="qpool", bufs=3))
         opool = ctx.enter_context(tc.tile_pool(name="opool", bufs=5))
         tps = ctx.enter_context(tc.psum_pool(name="tps", bufs=6))
@@ -73,7 +73,7 @@ def tile_irrepsstridelinear_kernel(tc, x, w0, w1, w2, w3, out):
 
         paired = {}
 
-        def pair_up(u):
+        def pair_up(u, gate):
             m, cp0, nb = UNITS[u]
             cp = cp0 + nb - 1
             pt = ppool.tile([P, 2, 2, P, 2], BF16, name="pairs", tag="pairs")
@@ -81,7 +81,7 @@ def tile_irrepsstridelinear_kernel(tc, x, w0, w1, w2, w3, out):
             for e in range(2):
                 nc.gpsimd.tensor_scalar(
                     out=pt[:, e], in0=src[:, 2 * cp + e],
-                    scalar1=1.0, scalar2=0.0, op0=ALU.mult, op1=ALU.add)
+                    scalar1=gate[:], scalar2=0.0, op0=ALU.mult, op1=ALU.add)
             paired[u] = pt
 
         def transposes(u):
@@ -163,11 +163,7 @@ def tile_irrepsstridelinear_kernel(tc, x, w0, w1, w2, w3, out):
 
         count = len(UNITS)
         transposes(0)
-        for k in range(FIRST_PAIRED, FIRST_PAIRED + AHEAD):
-            pair_up(k)
         for k in range(count + 2):
-            if FIRST_PAIRED + AHEAD <= k + 1 + AHEAD < count and k > 0:
-                pair_up(k + 1 + AHEAD)
             if k < count:
                 regroup(k)
             if k + 1 < count:
@@ -176,6 +172,10 @@ def tile_irrepsstridelinear_kernel(tc, x, w0, w1, w2, w3, out):
                 quantise_weights()
             if 0 <= k - 1 < count:
                 quantise(k - 1)
+                if k + AHEAD < count:
+                    gate = gates.tile([P, 1], F32, name="gate", tag="gate")
+                    nc.vector.memset(gate[:], 1.0)
+                    pair_up(k + AHEAD, gate)
                 multiply(k - 1)
             if 0 <= k - 2 < count:
                 drain(k - 2)

@@ -15,7 +15,7 @@ N, MI, MO, C = 1024, 512, 128, 16
 PACK = 4
 NT = N // P
 DEGREE = [0, 1, 1, 1, 2, 2, 2, 2, 2, 3, 3, 3, 3, 3, 3, 3]
-AHEAD = 3
+PAIRED = [u for u in range(5, 15, 2)] + [16]
 BANK = 2 * P * PACK
 
 FLOPS = 2 * N * C * MI * MO
@@ -30,7 +30,7 @@ def tile_irrepsstridelinear_kernel(tc, x, w0, w1, w2, w3, out):
         const = ctx.enter_context(tc.tile_pool(name="const", bufs=1))
         xpool = ctx.enter_context(tc.tile_pool(name="xpool", bufs=1))
         gpool = ctx.enter_context(tc.tile_pool(name="gpool", bufs=3))
-        ppool = ctx.enter_context(tc.tile_pool(name="ppool", bufs=6))
+        ppool = ctx.enter_context(tc.tile_pool(name="ppool", bufs=3))
         gates = ctx.enter_context(tc.tile_pool(name="gates", bufs=4))
         qpool = ctx.enter_context(tc.tile_pool(name="qpool", bufs=3))
         opool = ctx.enter_context(tc.tile_pool(name="opool", bufs=5))
@@ -73,16 +73,15 @@ def tile_irrepsstridelinear_kernel(tc, x, w0, w1, w2, w3, out):
 
         paired = {}
 
-        def pair_up(u, gate):
+        def pair_up(u, v, gate):
             m, cp0, nb = UNITS[u]
-            cp = cp0 + nb - 1
-            pt = ppool.tile([P, 2, 2, P, 2], BF16, name="pairs", tag="pairs")
-            src = xs[m][:].rearrange("n (p v s c) -> n c v p s", v=2, s=2, c=C)
-            for e in range(2):
-                nc.gpsimd.tensor_scalar(
-                    out=pt[:, e], in0=src[:, 2 * cp + e],
-                    scalar1=gate[:], scalar2=0.0, op0=ALU.mult, op1=ALU.add)
-            paired[u] = pt
+            c0 = 2 * (cp0 + nb - 2)
+            if v == 0:
+                paired[u] = ppool.tile([P, 4, 2, P, 2], BF16, name="pairs", tag="pairs")
+            src = xs[m][:].rearrange("n (p v s c) -> n v p s c", v=2, s=2, c=C)[:, v, :, :, c0:c0 + 4]
+            nc.gpsimd.tensor_scalar(
+                out=paired[u][:].rearrange("n c v p s -> n v p s c")[:, v], in0=src,
+                scalar1=gate[:], scalar2=0.0, op0=ALU.mult, op1=ALU.add)
 
         def transposes(u):
             m, cp0, nb = UNITS[u]
@@ -91,8 +90,9 @@ def tile_irrepsstridelinear_kernel(tc, x, w0, w1, w2, w3, out):
                 bank = tps.tile([P, PACK * P], F32, name="bank", tag="bank")
                 banks[(u, b)] = bank
                 for t in range(PACK):
-                    if u in paired and b == nb - 1:
-                        src = paired[u][:].rearrange("n e v p s -> n (e v p s)").bitcast(F32)[:, t * P:(t + 1) * P]
+                    if u in paired and b >= nb - 2:
+                        w0 = (b - nb + 2) * PACK + t
+                        src = paired[u][:].rearrange("n c v p s -> n (c v p s)").bitcast(F32)[:, w0 * P:(w0 + 1) * P]
                     else:
                         first = 8 * t + cp0 + b
                         src = words[:, first:first + 8 * PACK * (P - 1) + 1:8 * PACK]
@@ -104,14 +104,14 @@ def tile_irrepsstridelinear_kernel(tc, x, w0, w1, w2, w3, out):
             grouped[u] = g
             for b in range(nb):
                 part = g[:, b * BANK:(b + 1) * BANK]
-                if u in paired and b == nb - 1:
+                if u in paired and b >= nb - 2:
                     src = banks[(u, b)][:].rearrange("p (e v n) -> p e n v", e=2, v=2)
                     dst = part.bitcast(F32).rearrange("p (e n v) -> p e n v", e=2, v=2)
                 else:
                     src = banks[(u, b)][:].bitcast(BF16).rearrange(
                         "p (t n e) -> p e n t", t=PACK, n=P, e=2)
                     dst = part.rearrange("p (e n t) -> p e n t", e=2, n=P, t=PACK)
-                if (b + u) % 2 == 0:
+                if b % 2 == 0:
                     nc.vector.tensor_copy(out=dst, in_=src)
                 else:
                     nc.scalar.copy(out=dst, in_=src)
@@ -172,10 +172,10 @@ def tile_irrepsstridelinear_kernel(tc, x, w0, w1, w2, w3, out):
                 quantise_weights()
             if 0 <= k - 1 < count:
                 quantise(k - 1)
-                if k + AHEAD < count:
+                if k <= 2 * len(PAIRED):
                     gate = gates.tile([P, 1], F32, name="gate", tag="gate")
                     nc.vector.memset(gate[:], 1.0)
-                    pair_up(k + AHEAD, gate)
+                    pair_up(PAIRED[(k - 1) // 2], (k - 1) % 2, gate)
                 multiply(k - 1)
             if 0 <= k - 2 < count:
                 drain(k - 2)

@@ -15,12 +15,16 @@ N, MI, MO, C = 1024, 512, 128, 16
 PACK = 4
 NT = N // P
 DEGREE = [0, 1, 1, 1, 2, 2, 2, 2, 2, 3, 3, 3, 3, 3, 3, 3]
-PAIRED = [u for u in range(5, 15, 2)] + [16]
+PAIRED = [5, 7, 9]
+PIECES = [(u, v) for u in PAIRED for v in range(2)] + [(h, q) for h in range(2) for q in range(4)]
 BANK = 2 * P * PACK
 
 FLOPS = 2 * N * C * MI * MO
 
 UNITS = [(m, 4 * h, 4) for m in range(NT - 1) for h in range(2)] + [(NT - 1, 0, 4), (NT - 1, 4, 2), (NT - 1, 6, 2)]
+TURNED = 2 * (NT - 1)
+HN = P // 2
+DIRECT_AFTER = [4, 5]
 
 
 def tile_irrepsstridelinear_kernel(tc, x, w0, w1, w2, w3, out):
@@ -38,15 +42,24 @@ def tile_irrepsstridelinear_kernel(tc, x, w0, w1, w2, w3, out):
         ops = ctx.enter_context(tc.psum_pool(name="ops", bufs=2))
 
         xs = []
+        direct = []
         wraw = const.tile([P, 4, PACK, MO], BF16, name="wraw")
-        for m in range(NT):
-            xt = xpool.tile([P, MI * C], BF16, name="x%d" % m)
+        for m in range(NT - 1):
+            xt = xpool.tile([P, MI * C], BF16, name="x%d" % m, align_bytes=64)
             rows = x[m * P:(m + 1) * P].rearrange("n i c -> n (i c)")
             nc.sync.dma_start(out=xt[:], in_=rows)
             xs.append(xt)
             if m == 0:
                 for l, w in enumerate([w0, w1, w2, w3]):
                     nc.sync.dma_start(out=wraw[:, l], in_=w.rearrange("(p j) o -> p j o", j=PACK))
+            if m in DIRECT_AFTER:
+                h = DIRECT_AFTER.index(m)
+                dt = xpool.tile([P, HN, PACK, C], BF16, name="d%d" % h)
+                n0 = (NT - 1) * P + h * HN
+                nc.sync.dma_start(
+                    out=dt[:].rearrange("p n t c -> p n (t c)"),
+                    in_=x[n0:n0 + HN].rearrange("n (p t) c -> p n (t c)", t=PACK))
+                direct.append(dt)
 
         ident = const.tile([P, P], F32, name="ident")
         make_identity(nc, ident[:])
@@ -72,6 +85,15 @@ def tile_irrepsstridelinear_kernel(tc, x, w0, w1, w2, w3, out):
         staged = {}
 
         paired = {}
+        lastg = []
+
+        def spread(h, q, gate):
+            if not lastg:
+                lastg.append(xpool.tile([P, C, 2, HN * PACK], BF16, name="x0", tag="x0", align_bytes=64))
+            nc.gpsimd.tensor_scalar(
+                out=lastg[0][:, 4 * q:4 * q + 4, h].rearrange("p c f -> p f c"),
+                in0=direct[h][:].rearrange("p n t c -> p (n t) c")[:, :, 4 * q:4 * q + 4],
+                scalar1=gate[:], scalar2=0.0, op0=ALU.mult, op1=ALU.add)
 
         def pair_up(u, v, gate):
             m, cp0, nb = UNITS[u]
@@ -123,7 +145,8 @@ def tile_irrepsstridelinear_kernel(tc, x, w0, w1, w2, w3, out):
             wide = nb * BANK // PACK
             nc.vector.quantize_mx(
                 out=codes[:, :wide].bitcast(FP8X4), scales=scales[:, :wide],
-                in_=grouped[u][:, :nb * BANK])
+                in_=grouped[u][:, :nb * BANK] if u < TURNED else
+                lastg[0][:].rearrange("p c h f -> p (c h f)")[:, cp0 * BANK:(cp0 + nb) * BANK])
             quant[u] = (codes, scales)
 
         def multiply(u):
@@ -164,18 +187,22 @@ def tile_irrepsstridelinear_kernel(tc, x, w0, w1, w2, w3, out):
         count = len(UNITS)
         transposes(0)
         for k in range(count + 2):
-            if k < count:
+            if k < TURNED:
                 regroup(k)
-            if k + 1 < count:
+            if k + 1 < TURNED:
                 transposes(k + 1)
             if k == 1:
                 quantise_weights()
             if 0 <= k - 1 < count:
                 quantise(k - 1)
-                if k <= 2 * len(PAIRED):
+                if k <= len(PIECES):
+                    a, b = PIECES[k - 1]
                     gate = gates.tile([P, 1], F32, name="gate", tag="gate")
                     nc.vector.memset(gate[:], 1.0)
-                    pair_up(PAIRED[(k - 1) // 2], (k - 1) % 2, gate)
+                    if k <= 2 * len(PAIRED):
+                        pair_up(a, b, gate)
+                    else:
+                        spread(a, b, gate)
                 multiply(k - 1)
             if 0 <= k - 2 < count:
                 drain(k - 2)

@@ -16,7 +16,7 @@ PACK = 4
 NT = N // P
 DEGREE = [0, 1, 1, 1, 2, 2, 2, 2, 2, 3, 3, 3, 3, 3, 3, 3]
 PAIRED = [5, 7, 9]
-PIECES = [(u, v) for u in PAIRED for v in range(2)] + [(h, q) for h in range(2) for q in range(4)]
+PIECES = [(u, v) for u in PAIRED for v in range(2)] + [(0, q) for q in range(4)] + [(1, q) for q in range(2)]
 BANK = 2 * P * PACK
 
 FLOPS = 2 * N * C * MI * MO
@@ -24,7 +24,7 @@ FLOPS = 2 * N * C * MI * MO
 UNITS = [(m, 4 * h, 4) for m in range(NT - 1) for h in range(2)] + [(NT - 1, 0, 4), (NT - 1, 4, 2), (NT - 1, 6, 2)]
 TURNED = 2 * (NT - 1)
 HN = P // 2
-DIRECT_AFTER = [4, 5]
+DIRECT_AFTER = [4, 6]
 
 
 def tile_irrepsstridelinear_kernel(tc, x, w0, w1, w2, w3, out):
@@ -90,10 +90,13 @@ def tile_irrepsstridelinear_kernel(tc, x, w0, w1, w2, w3, out):
         def spread(h, q, gate):
             if not lastg:
                 lastg.append(xpool.tile([P, C, 2, HN * PACK], BF16, name="x0", tag="x0", align_bytes=64))
-            nc.gpsimd.tensor_scalar(
-                out=lastg[0][:, 4 * q:4 * q + 4, h].rearrange("p c f -> p f c"),
-                in0=direct[h][:].rearrange("p n t c -> p (n t) c")[:, :, 4 * q:4 * q + 4],
-                scalar1=gate[:], scalar2=0.0, op0=ALU.mult, op1=ALU.add)
+            dst = lastg[0][:, 4 * q:4 * q + 4, h].rearrange("p c f -> p f c")
+            src = direct[h][:].rearrange("p n t c -> p (n t) c")[:, :, 4 * q:4 * q + 4]
+            if gate is None:
+                nc.vector.tensor_copy(out=dst, in_=src)
+            else:
+                nc.gpsimd.tensor_scalar(
+                    out=dst, in0=src, scalar1=gate[:], scalar2=0.0, op0=ALU.mult, op1=ALU.add)
 
         def pair_up(u, v, gate):
             m, cp0, nb = UNITS[u]
@@ -203,6 +206,9 @@ def tile_irrepsstridelinear_kernel(tc, x, w0, w1, w2, w3, out):
                         pair_up(a, b, gate)
                     else:
                         spread(a, b, gate)
+                if k == TURNED:
+                    for q in (2, 3):
+                        spread(1, q, None)
                 multiply(k - 1)
             if 0 <= k - 2 < count:
                 drain(k - 2)

from contextlib import ExitStack

import concourse.mybir as mybir
from concourse.masks import make_identity

F32 = mybir.dt.float32
BF16 = mybir.dt.bfloat16
U32 = mybir.dt.uint32
U8 = mybir.dt.uint8
FP8X4 = mybir.dt.float8_e4m3fn_x4
ALU = mybir.AluOpType

P = 128
N, MI, MO, C = 1024, 512, 128, 16
PACK = 4
NT = N // P
DEGREE = [0, 1, 1, 1, 2, 2, 2, 2, 2, 3, 3, 3, 3, 3, 3, 3]
PAIRED = [5, 7, 9]
PIECES = [(u, v) for u in PAIRED for v in range(2)] + [(0, q) for q in range(4)] + [(1, q) for q in range(2)]
BANK = 2 * P * PACK

FLOPS = 2 * N * C * MI * MO

UNITS = [(m, 4 * h, 4) for m in range(NT - 1) for h in range(2)] + [(NT - 1, 0, 4), (NT - 1, 4, 2), (NT - 1, 6, 2)]
TURNED = 2 * (NT - 1)
HN = P // 2
DIRECT_AFTER = [4, 6]


def tile_irrepsstridelinear_kernel(tc, x, w0, w1, w2, w3, out):
    nc = tc.nc
    with ExitStack() as ctx:
        ctx.enter_context(tc.manual_schedule())
        const = ctx.enter_context(tc.tile_pool(name="const", bufs=1))
        xpool = ctx.enter_context(tc.tile_pool(name="xpool", bufs=1))
        gpool = ctx.enter_context(tc.tile_pool(name="gpool", bufs=3))
        ppool = ctx.enter_context(tc.tile_pool(name="ppool", bufs=3))
        gates = ctx.enter_context(tc.tile_pool(name="gates", bufs=4))
        qpool = ctx.enter_context(tc.tile_pool(name="qpool", bufs=3))
        opool = ctx.enter_context(tc.tile_pool(name="opool", bufs=5))
        tps = ctx.enter_context(tc.psum_pool(name="tps", bufs=6))
        ops = ctx.enter_context(tc.psum_pool(name="ops", bufs=2))

        xs = []
        direct = []
        wraw = const.tile([P, 4, PACK, MO], BF16, name="wraw")
        for m in range(NT - 1):
            xt = xpool.tile([P, MI * C], BF16, name="x%d" % m, align_bytes=64)
            rows = x[m * P:(m + 1) * P].rearrange("n i c -> n (i c)")
            nc.sync.dma_start(out=xt[:], in_=rows)
            xs.append(xt)
            if m == 0:
                for l, w in enumerate([w0, w1, w2, w3]):
                    nc.sync.dma_start(out=wraw[:, l], in_=w.rearrange("(p j) o -> p j o", j=PACK))
            if m in DIRECT_AFTER:
                h = DIRECT_AFTER.index(m)
                dt = xpool.tile([P, HN, PACK, C], BF16, name="d%d" % h)
                n0 = (NT - 1) * P + h * HN
                nc.sync.dma_start(
                    out=dt[:].rearrange("p n t c -> p n (t c)"),
                    in_=x[n0:n0 + HN].rearrange("n (p t) c -> p n (t c)", t=PACK))
                direct.append(dt)

        ident = const.tile([P, P], F32, name="ident")
        make_identity(nc, ident[:])

        wgrp = const.tile([P, 4, MO, PACK], BF16, name="wgrp", align_bytes=64)
        wcodes = const.tile([P, 4 * MO], U32, name="wcodes", align_bytes=64)
        wscales = const.tile([P, 4 * MO], U8, name="wscales", align_bytes=64)
        nc.gpsimd.tensor_scalar(
            out=wgrp[:], in0=wraw[:].rearrange("p l j o -> p l o j"),
            scalar1=1.0, scalar2=0.0, op0=ALU.mult, op1=ALU.add)

        def quantise_weights():
            nc.vector.quantize_mx(
                out=wcodes[:].bitcast(FP8X4),
                scales=wscales[:],
                in_=wgrp[:].rearrange("p l o j -> p (l o j)"),
            )

        banks = {}
        grouped = {}
        quant = {}
        accs = {}
        staged = {}

        paired = {}
        lastg = []

        def spread(h, q, gate):
            if not lastg:
                lastg.append(xpool.tile([P, C, 2, HN * PACK], BF16, name="x0", tag="x0", align_bytes=64))
            dst = lastg[0][:, 4 * q:4 * q + 4, h].rearrange("p c f -> p f c")
            src = direct[h][:].rearrange("p n t c -> p (n t) c")[:, :, 4 * q:4 * q + 4]
            if gate is None:
                nc.vector.tensor_copy(out=dst, in_=src)
            else:
                nc.gpsimd.tensor_scalar(
                    out=dst, in0=src, scalar1=gate[:], scalar2=0.0, op0=ALU.mult, op1=ALU.add)

        def pair_up(u, v, gate):
            m, cp0, nb = UNITS[u]
            c0 = 2 * (cp0 + nb - 2)
            if v == 0:
                paired[u] = ppool.tile([P, 4, 2, P, 2], BF16, name="pairs", tag="pairs")
            src = xs[m][:].rearrange("n (p v s c) -> n v p s c", v=2, s=2, c=C)[:, v, :, :, c0:c0 + 4]
            nc.gpsimd.tensor_scalar(
                out=paired[u][:].rearrange("n c v p s -> n v p s c")[:, v], in0=src,
                scalar1=gate[:], scalar2=0.0, op0=ALU.mult, op1=ALU.add)

        def transposes(u):
            m, cp0, nb = UNITS[u]
            words = xs[m][:].bitcast(F32)
            for b in range(nb):
                bank = tps.tile([P, PACK * P], F32, name="bank", tag="bank")
                banks[(u, b)] = bank
                for t in range(PACK):
                    if u in paired and b >= nb - 2:
                        w0 = (b - nb + 2) * PACK + t
                        src = paired[u][:].rearrange("n c v p s -> n (c v p s)").bitcast(F32)[:, w0 * P:(w0 + 1) * P]
                    else:
                        first = 8 * t + cp0 + b
                        src = words[:, first:first + 8 * PACK * (P - 1) + 1:8 * PACK]
                    nc.tensor.transpose(bank[:, t * P:(t + 1) * P], src, ident[:])

        def regroup(u):
            m, cp0, nb = UNITS[u]
            g = gpool.tile([P, 4 * BANK], BF16, name="g", tag="g", align_bytes=64)
            grouped[u] = g
            for b in range(nb):
                part = g[:, b * BANK:(b + 1) * BANK]
                if u in paired and b >= nb - 2:
                    src = banks[(u, b)][:].rearrange("p (e v n) -> p e n v", e=2, v=2)
                    dst = part.bitcast(F32).rearrange("p (e n v) -> p e n v", e=2, v=2)
                else:
                    src = banks[(u, b)][:].bitcast(BF16).rearrange(
                        "p (t n e) -> p e n t", t=PACK, n=P, e=2)
                    dst = part.rearrange("p (e n t) -> p e n t", e=2, n=P, t=PACK)
                if b % 2 == 0:
                    nc.vector.tensor_copy(out=dst, in_=src)
                else:
                    nc.scalar.copy(out=dst, in_=src)

        def quantise(u):
            m, cp0, nb = UNITS[u]
            codes = qpool.tile([P, BANK], U32, name="codes", tag="codes", align_bytes=64)
            scales = qpool.tile([P, BANK], U8, name="scales", tag="scales", align_bytes=64)
            wide = nb * BANK // PACK
            nc.vector.quantize_mx(
                out=codes[:, :wide].bitcast(FP8X4), scales=scales[:, :wide],
                in_=grouped[u][:, :nb * BANK] if u < TURNED else
                lastg[0][:].rearrange("p c h f -> p (c h f)")[:, cp0 * BANK:(cp0 + nb) * BANK])
            quant[u] = (codes, scales)

        def multiply(u):
            m, cp0, nb = UNITS[u]
            codes, scales = quant[u]
            for b in range(nb // 2):
                acc = ops.tile([P, 4 * MO], F32, name="acc", tag="acc")
                for cc in range(4):
                    cl = 4 * b + cc
                    l = DEGREE[2 * cp0 + cl]
                    nc.tensor.matmul_mx(
                        out=acc[:, cc * MO:(cc + 1) * MO],
                        lhsT=codes[:, cl * P:(cl + 1) * P].bitcast(FP8X4),
                        lhsT_scale=scales[:, cl * P:(cl + 1) * P],
                        rhs=wcodes[:, l * MO:(l + 1) * MO].bitcast(FP8X4),
                        rhs_scale=wscales[:, l * MO:(l + 1) * MO],
                        start=True,
                        stop=True,
                    )
                accs[(u, b)] = acc

        def drain(u):
            m, cp0, nb = UNITS[u]
            if cp0 == 0:
                staged[m] = opool.tile([P, MO * C], F32, name="osb", tag="osb")
            osb = staged[m]
            view = osb[:].rearrange("p (o c) -> p o c", c=C)
            for b in range(nb // 2):
                c0 = 2 * cp0 + 4 * b
                nc.scalar.copy(
                    out=view[:, :, c0:c0 + 4],
                    in_=accs[(u, b)][:].rearrange("p (cc o) -> p o cc", cc=4),
                )
            if cp0 + nb == C // 2:
                nc.sync.dma_start(
                    out=out[m * P:(m + 1) * P].rearrange("n o c -> n (o c)"), in_=osb[:])

        count = len(UNITS)
        transposes(0)
        for k in range(count + 2):
            if k < TURNED:
                regroup(k)
            if k + 1 < TURNED:
                transposes(k + 1)
            if k == 1:
                quantise_weights()
            if 0 <= k - 1 < count:
                quantise(k - 1)
                if k <= len(PIECES):
                    a, b = PIECES[k - 1]
                    gate = gates.tile([P, 1], F32, name="gate", tag="gate")
                    nc.vector.memset(gate[:], 1.0)
                    if k <= 2 * len(PAIRED):
                        pair_up(a, b, gate)
                    else:
                        spread(a, b, gate)
                if k == TURNED:
                    for q in (2, 3):
                        spread(1, q, None)
                multiply(k - 1)
            if 0 <= k - 2 < count:
                drain(k - 2)
